import numpy as np
import ml_dtypes


def mxq(x, axis, fmt="e4m3"):
    dtype, down = {"e4m3": (ml_dtypes.float8_e4m3fn, 7), "e5m2": (ml_dtypes.float8_e5m2, 14)}[fmt]
    v = np.moveaxis(np.asarray(x, np.float32).astype(ml_dtypes.bfloat16).astype(np.float64), axis, -1)
    blocks = v.reshape(v.shape[:-1] + (-1, 32))
    amax = np.abs(blocks).max(-1, keepdims=True)
    byte = np.maximum(np.where(amax > 0, np.frexp(amax)[1] - 1 + 127, 0) - down, 1)
    scale = np.exp2(byte - 127.0)
    codes = (blocks / scale).astype(np.float32).astype(dtype).astype(np.float64)
    return np.moveaxis((codes * scale).reshape(v.shape), -1, axis)


WIDE = False


def mx_kscale(k):
    if not WIDE:
        return np.ones(k)
    levels = np.array([18, -18])
    if k % 512:
        return np.exp2(np.random.permutation(np.resize(levels, k // 32))).repeat(32)
    a = np.empty((k // 512, 16))
    for p in range(k // 512):
        a[p, :8] = np.random.permutation(np.resize(levels, 8))
        for g in range(8):
            far = levels[np.abs(levels - a[p, g]) >= 10]
            a[p, g + 8] = far[np.random.randint(len(far))]
    return np.exp2(a.ravel()).repeat(32)


BF16 = ml_dtypes.bfloat16


def bf(x):
    return np.asarray(x, np.float32).astype(BF16)


def f64(x):
    return np.asarray(x).astype(np.float64)


N, F, NB = 1024, 512, 32


def setup_inputs():
    u = mx_kscale(N)
    t = mx_kscale(N)
    s = np.concatenate([u[:N // 2], t[N // 2:]])
    v = mx_kscale(F)
    edge = np.random.random_sample((N, N)) < NB / N
    h0 = bf(np.random.standard_normal((N, F)))
    adj0 = bf(np.random.random_sample((N, N)) * edge)
    W2_0 = bf(np.random.standard_normal((F, F)) * 2.0 / np.sqrt(F))
    b2 = bf(np.random.standard_normal(F) * 0.2)
    g = bf(4.0 * np.random.standard_normal((N, F)) * np.exp2(np.random.randint(-6, 1, (N, 1))) / s[:, None] * v[None, :])
    dinv = (f64(adj0).sum(axis=1) + 1.0) ** -0.5
    return {"h_ln": bf(f64(h0) * s[:, None]),
            "adj": bf(f64(adj0) * s[:, None] / s[None, :]),
            "W2": bf(f64(W2_0) / v[None, :]),
            "b2": b2,
            "dinv": np.asarray(dinv, np.float32),
            "grad_out": g}


def reference(h_ln, adj, W2, b2, dinv, grad_out):
    d = f64(dinv)[:, None]
    dz2 = d * f64(grad_out)
    dhs = (mxq(f64(adj), 0, "e4m3").T @ mxq(dz2, 0, "e5m2")) + dz2
    dz1 = d * dhs
    dx = mxq(dz1, 1, "e5m2") @ mxq(f64(W2), 1, "e4m3").T
    dw = mxq(f64(h_ln), 0, "e4m3").T @ mxq(dz1, 0, "e5m2")
    return dx, dw

@@ -1,0 +1,293 @@
+from contextlib import ExitStack
+
+import concourse.mybir as mybir
+from concourse.masks import make_identity
+
+N, F = 1024, 512
+FLOPS = 2 * N * N * F + 2 * N * F * F + 2 * N * F * F
+BYTES = 2 * (N * F + N * N + F * F + N * F) + 4 * N + 4 * (N * F + F * F)
+
+F32 = mybir.dt.float32
+BF16 = mybir.dt.bfloat16
+U32 = mybir.dt.uint32
+U8 = mybir.dt.uint8
+E4M3 = mybir.dt.float8_e4m3fn_x4
+E5M2 = mybir.dt.float8_e5m2_x4
+MULT = mybir.AluOpType.mult
+ADD = mybir.AluOpType.add
+COPY = mybir.ActivationFunctionType.Copy
+
+P = 128
+PACK = 4
+K_PASS = P * PACK
+GROUPS = N // K_PASS
+WIDE = PACK * F
+
+
+def tile_gcnlayer_pb_v_kernel(tc, h_ln, adj, W2, b2, dinv, grad_out, out_0, out_1):
+    nc = tc.nc
+    with ExitStack() as ctx:
+        sb = ctx.enter_context(tc.tile_pool(name="sb", bufs=1))
+        ps = ctx.enter_context(tc.psum_pool(name="ps", bufs=1))
+        ctx.enter_context(tc.manual_schedule())
+
+        def wide(name, dtype=BF16):
+            return sb.tile([P, WIDE], dtype, name=name, align_bytes=64)
+
+        def operand(name, fmt):
+            codes = sb.tile([P, F], U32, name=name + "_codes", align_bytes=64)
+            scales = sb.tile([P, F], U8, name=name + "_scales", align_bytes=64)
+            return {"values": wide(name + "_values"), "codes": codes, "scales": scales, "fmt": fmt}
+
+        bank = [ps.tile([P, F], F32, name="bank%d" % b) for b in range(8)]
+        ident_bf16 = sb.tile([P, P], BF16, name="ident_bf16")
+        ident = sb.tile([P, P], F32, name="ident")
+        d = sb.tile([P, GROUPS * PACK], F32, name="d")
+        d_sq = sb.tile([P, GROUPS * PACK], F32, name="d_sq")
+        g_raw = [wide("g_raw%d" % g) for g in range(GROUPS)]
+        h_raw = [wide("h_raw%d" % g) for g in range(GROUPS)]
+        adj_raw = [[wide("adj_raw%d%d" % (i, j)) for j in range(GROUPS)] for i in range(GROUPS)]
+        w_raw = wide("w_raw")
+        dz2 = [wide("dz2_%d" % g) for g in range(GROUPS)]
+        loop_term = [wide("loop_term%d" % g, F32) for g in range(GROUPS)]
+        dz1 = [wide("dz1_%d" % g) for g in range(GROUPS)]
+        dx = [wide("dx%d" % g, F32) for g in range(GROUPS)]
+        dw = wide("dw", F32)
+        dz2_q = [operand("dz2_q%d" % g, E5M2) for g in range(GROUPS)]
+        adj_q = [[operand("adj_q%d%d" % (i, j), E4M3) for j in range(GROUPS)] for i in range(GROUPS)]
+        h_q = [operand("h_q%d" % g, E4M3) for g in range(GROUPS)]
+        w_q = operand("w_q", E4M3)
+        dz1_node_q = [operand("dz1_node_q%d" % g, E5M2) for g in range(GROUPS)]
+        dz1_feat_q = [operand("dz1_feat_q%d" % g, E5M2) for g in range(GROUPS)]
+
+        def slot(t):
+            return slice(t * F, (t + 1) * F)
+
+        def block(t):
+            return slice(t * P, (t + 1) * P)
+
+        def group_rows(g):
+            return slice(g * K_PASS, (g + 1) * K_PASS)
+
+        def load(tile, rows, slots=slice(0, PACK)):
+            nc.sync.dma_start(
+                out=tile[:].rearrange("p (t c) -> p t c", t=PACK)[:, slots],
+                in_=rows.rearrange("(p t) c -> p t c", t=PACK)[:, slots],
+            )
+
+        def copy_on(engine, out, in_):
+            if engine == "vector":
+                nc.vector.tensor_copy(out=out, in_=in_)
+            else:
+                nc.scalar.copy(out=out, in_=in_)
+
+        def in_halves(ap):
+            return ap.rearrange("p (w u e) -> p u w e", u=2, e=2)
+
+        def as_halves(ap):
+            return ap.rearrange("p (u w e) -> p u w e", u=2, e=2)
+
+        def scale_grad(g):
+            for t in range(PACK):
+                nc.vector.tensor_scalar(
+                    out=as_halves(dz2[g][:, slot(t)]),
+                    in0=in_halves(g_raw[g][:, slot(t)]),
+                    scalar1=d[:, g * PACK + t : g * PACK + t + 1],
+                    scalar2=None,
+                    op0=MULT,
+                )
+
+        def self_loop(g, slots):
+            for t in slots:
+                nc.scalar.activation(
+                    out=as_halves(loop_term[g][:, slot(t)]),
+                    in_=in_halves(g_raw[g][:, slot(t)]),
+                    func=COPY,
+                    scale=d_sq[:, g * PACK + t : g * PACK + t + 1],
+                )
+
+        def interleave(engine, q, src, runs=slice(0, P)):
+            copy_on(
+                engine,
+                q["values"][:].rearrange("p (c i t) -> p c t i", i=4, t=PACK)[:, runs],
+                src[:].rearrange("p (t c i) -> p c t i", i=4, t=PACK)[:, runs],
+            )
+
+        def interleave_adj(engine, i, j):
+            copy_on(
+                engine,
+                adj_q[i][j]["values"][:].rearrange("p (s a b t) -> p a s b t", s=PACK, b=2, t=PACK),
+                adj_raw[i][j][:].rearrange("p (t a b s) -> p a s b t", s=PACK, b=2, t=PACK),
+            )
+
+        def quantize(q, cols=slice(0, F)):
+            nc.vector.quantize_mx(
+                out=q["codes"][:, cols].bitcast(q["fmt"]),
+                scales=q["scales"][:, cols],
+                in_=q["values"][:, cols.start * PACK : cols.stop * PACK],
+            )
+
+        def matmul(b, lhs, cols, rhs, start, stop):
+            nc.tensor.matmul_mx(
+                out=bank[b][:],
+                lhsT=lhs["codes"][:, cols].bitcast(lhs["fmt"]),
+                lhsT_scale=lhs["scales"][:, cols],
+                rhs=rhs["codes"][:].bitcast(rhs["fmt"]),
+                rhs_scale=rhs["scales"][:],
+                start=start,
+                stop=stop,
+            )
+
+        def aggregate(i, j):
+            for t in range(PACK):
+                matmul(j * PACK + t, adj_q[i][j], block(t), dz2_q[i], i == 0, i == GROUPS - 1)
+
+        def make_dz1(g, t):
+            nc.vector.scalar_tensor_tensor(
+                out=dz1[g][:, slot(t)],
+                in0=bank[g * PACK + t][:],
+                scalar=d[:, g * PACK + t : g * PACK + t + 1],
+                in1=loop_term[g][:, slot(t)],
+                op0=MULT,
+                op1=ADD,
+            )
+
+        def transpose_w(half, b):
+            words = w_raw[:].bitcast(F32)
+            for r in range(2):
+                base = (2 * half + r) * 2 * P
+                for u in range(2):
+                    nc.tensor.transpose(bank[b][:, block(2 * r + u)], words[:, base + u : base + 2 * P : 2], ident[:])
+
+        def collect_w(half, b):
+            nc.scalar.copy(
+                out=w_q["values"][:].bitcast(F32).rearrange("p (n r u) -> p n r u", r=PACK, u=2)[:, :, 2 * half : 2 * half + 2, :],
+                in_=bank[b][:].rearrange("p (r u n) -> p n r u", r=2, u=2),
+            )
+
+        def transpose_dz1(g, half, b):
+            words = dz1[g][:].bitcast(F32)
+            for r in range(PACK):
+                nc.tensor.transpose(bank[b][:, block(r)], words[:, block(PACK * half + r)], ident[:])
+
+        def collect_dz1(g, half, b):
+            nc.scalar.copy(
+                out=dz1_feat_q[g]["values"][:].bitcast(F32)[:, slot(half)].rearrange("p (t n u) -> p t n u", t=2, u=2),
+                in_=bank[b][:].rearrange("p (t u n) -> p t n u", t=2, u=2),
+            )
+
+        def dx_matmul(g, t, b):
+            matmul(b, dz1_feat_q[g], block(t), w_q, True, True)
+
+        def dx_out(engine, g, t, b):
+            copy_on(engine, dx[g][:, slot(t)], bank[b][:])
+            rows = out_0[group_rows(g), :].rearrange("(p t) c -> p t c", t=PACK)
+            nc.sync.dma_start(out=rows[:, t, :], in_=dx[g][:, slot(t)])
+
+        def dw_matmul(g, r, b):
+            matmul(b, h_q[g], block(r), dz1_node_q[g], g == 0, g == GROUPS - 1)
+
+        def dw_out(engine, r, b):
+            copy_on(
+                engine,
+                dw[:, slot(r)].rearrange("p (w u e) -> p w u e", u=2, e=2),
+                bank[b][:].rearrange("p (u w e) -> p w u e", u=2, e=2),
+            )
+            nc.sync.dma_start(out=out_1[block(r), :], in_=dw[:, slot(r)])
+
+        nc.scalar.dma_start(
+            out=d[:].rearrange("p (g t) -> p g t", t=PACK),
+            in_=dinv.rearrange("(g p t) -> p g t", p=P, t=PACK),
+        )
+        load(g_raw[0], grad_out[group_rows(0), :], slice(0, 2))
+        load(g_raw[0], grad_out[group_rows(0), :], slice(2, 4))
+        load(adj_raw[0][0], adj[group_rows(0), group_rows(0)])
+        load(g_raw[1], grad_out[group_rows(1), :])
+        load(adj_raw[1][0], adj[group_rows(1), group_rows(0)])
+        load(adj_raw[0][1], adj[group_rows(0), group_rows(1)])
+        load(w_raw, W2)
+        load(adj_raw[1][1], adj[group_rows(1), group_rows(1)])
+        load(h_raw[0], h_ln[group_rows(0), :])
+        load(h_raw[1], h_ln[group_rows(1), :])
+        make_identity(nc, ident_bf16[:])
+        nc.scalar.activation(out=ident[:], in_=ident_bf16[:], func=COPY)
+        nc.vector.tensor_tensor(out=d_sq[:], in0=d[:], in1=d[:], op=MULT)
+
+        scale_grad(0)
+        self_loop(0, range(PACK))
+        interleave("vector", dz2_q[0], dz2[0])
+        interleave_adj("vector", 0, 0)
+        self_loop(1, (0, 1))
+        quantize(dz2_q[0])
+        scale_grad(1)
+        quantize(adj_q[0][0])
+        aggregate(0, 0)
+        interleave_adj("scalar", 1, 0)
+        interleave("vector", dz2_q[1], dz2[1])
+        quantize(adj_q[1][0])
+        quantize(dz2_q[1])
+        interleave_adj("scalar", 0, 1)
+        transpose_w(0, 4)
+        transpose_w(1, 5)
+        aggregate(1, 0)
+        interleave_adj("vector", 1, 1)
+        collect_w(0, 4)
+        collect_w(1, 5)
+        self_loop(1, (2, 3))
+        quantize(adj_q[0][1])
+        aggregate(0, 1)
+        make_dz1(0, 0)
+        quantize(adj_q[1][1])
+        make_dz1(0, 1)
+        aggregate(1, 1)
+        transpose_dz1(0, 0, 0)
+        interleave("scalar", h_q[0], h_raw[0])
+        make_dz1(0, 2)
+        make_dz1(0, 3)
+        transpose_dz1(0, 1, 1)
+        interleave("scalar", h_q[1], h_raw[1], slice(0, 48))
+        collect_dz1(0, 0, 0)
+        collect_dz1(0, 1, 1)
+        quantize(w_q)
+        make_dz1(1, 0)
+        make_dz1(1, 1)
+        quantize(dz1_feat_q[0], slice(0, 256))
+        dx_matmul(0, 0, 2)
+        dx_matmul(0, 1, 3)
+        transpose_dz1(1, 0, 4)
+        make_dz1(1, 2)
+        quantize(dz1_feat_q[0], slice(256, 512))
+        dx_matmul(0, 2, 0)
+        dx_matmul(0, 3, 1)
+        make_dz1(1, 3)
+        transpose_dz1(1, 1, 5)
+        interleave("scalar", h_q[1], h_raw[1], slice(48, 80))
+        for t in range(PACK):
+            dx_out("scalar", 0, t, (t + 2) % 4)
+        collect_dz1(1, 0, 4)
+        collect_dz1(1, 1, 5)
+        interleave("vector", dz1_node_q[0], dz1[0])
+        quantize(h_q[0])
+        quantize(dz1_feat_q[1], slice(0, 256))
+        dx_banks = (6, 7, 2, 3)
+        dx_matmul(1, 0, dx_banks[0])
+        dx_matmul(1, 1, dx_banks[1])
+        quantize(dz1_node_q[0])
+        quantize(dz1_feat_q[1], slice(256, 512))
+        dx_matmul(1, 2, dx_banks[2])
+        dx_matmul(1, 3, dx_banks[3])
+        dw_banks = (0, 1, 4, 5)
+        for r in range(PACK):
+            dw_matmul(0, r, dw_banks[r])
+        interleave("scalar", h_q[1], h_raw[1], slice(80, 128))
+        interleave("vector", dz1_node_q[1], dz1[1])
+        for t in range(PACK):
+            dx_out("scalar", 1, t, dx_banks[t])
+        quantize(h_q[1], block(0))
+        quantize(dz1_node_q[1])
+        for r in range(PACK):
+            dw_matmul(1, r, dw_banks[r])
+            if r + 1 < PACK:
+                quantize(h_q[1], block(r + 1))
+        for r in range(PACK):
+            dw_out("scalar" if r % 2 == 0 else "vector", r, dw_banks[r])

@@ -34,10 +34,11 @@ def tile_gcnlayer_pb_v_kernel(tc, h_ln, adj, W2, b2, dinv, grad_out, out_0, out_
         def wide(name, dtype=BF16):
             return sb.tile([P, WIDE], dtype, name=name, align_bytes=64)
 
-        def operand(name, fmt):
-            codes = sb.tile([P, F], U32, name=name + "_codes", align_bytes=64)
-            scales = sb.tile([P, F], U8, name=name + "_scales", align_bytes=64)
-            return {"values": wide(name + "_values"), "codes": codes, "scales": scales, "fmt": fmt}
+        def operand(name, fmt, columns=F):
+            values = sb.tile([P, columns * PACK], BF16, name=name + "_values", align_bytes=64)
+            codes = sb.tile([P, columns], U32, name=name + "_codes", align_bytes=64)
+            scales = sb.tile([P, columns], U8, name=name + "_scales", align_bytes=64)
+            return {"values": values, "codes": codes, "scales": scales, "fmt": fmt}
 
         bank = [ps.tile([P, F], F32, name="bank%d" % b) for b in range(8)]
         ident_bf16 = sb.tile([P, P], BF16, name="ident_bf16")
@@ -55,7 +56,7 @@ def tile_gcnlayer_pb_v_kernel(tc, h_ln, adj, W2, b2, dinv, grad_out, out_0, out_
         dw = wide("dw", F32)
         dz2_q = [operand("dz2_q%d" % g, E5M2) for g in range(GROUPS)]
         adj_q = [[operand("adj_q%d%d" % (i, j), E4M3) for j in range(GROUPS)] for i in range(GROUPS)]
-        h_q = [operand("h_q%d" % g, E4M3) for g in range(GROUPS)]
+        h_q = operand("h_q", E4M3, GROUPS * F)
         w_q = operand("w_q", E4M3)
         dz1_node_q = [operand("dz1_node_q%d" % g, E5M2) for g in range(GROUPS)]
         dz1_feat_q = [operand("dz1_feat_q%d" % g, E5M2) for g in range(GROUPS)]
@@ -118,6 +119,13 @@ def tile_gcnlayer_pb_v_kernel(tc, h_ln, adj, W2, b2, dinv, grad_out, out_0, out_
                 engine,
                 adj_q[i][j]["values"][:].rearrange("p (s a b t) -> p a s b t", s=PACK, b=2, t=PACK),
                 adj_raw[i][j][:].rearrange("p (t a b s) -> p a s b t", s=PACK, b=2, t=PACK),
+            )
+
+        def interleave_h(engine, g, blocks):
+            copy_on(
+                engine,
+                h_q["values"][:].rearrange("p (r g c i t) -> p r g c t i", r=PACK, g=GROUPS, i=4, t=PACK)[:, blocks, g],
+                h_raw[g][:].rearrange("p (t r c i) -> p r c t i", r=PACK, i=4, t=PACK)[:, blocks],
             )
 
         def quantize(q, cols=slice(0, F)):
@@ -184,8 +192,10 @@ def tile_gcnlayer_pb_v_kernel(tc, h_ln, adj, W2, b2, dinv, grad_out, out_0, out_
             rows = out_0[group_rows(g), :].rearrange("(p t) c -> p t c", t=PACK)
             nc.sync.dma_start(out=rows[:, t, :], in_=dx[g][:, slot(t)])
 
-        def dw_matmul(g, r, b):
-            matmul(b, h_q[g], block(r), dz1_node_q[g], g == 0, g == GROUPS - 1)
+        def dw_matmuls(r, b):
+            quantize(h_q, slice(r * GROUPS * P, (r + 1) * GROUPS * P))
+            for g in range(GROUPS):
+                matmul(b, h_q, block(r * GROUPS + g), dz1_node_q[g], g == 0, g == GROUPS - 1)
 
         def dw_out(engine, r, b):
             copy_on(
@@ -201,11 +211,11 @@ def tile_gcnlayer_pb_v_kernel(tc, h_ln, adj, W2, b2, dinv, grad_out, out_0, out_
         )
         load(g_raw[0], grad_out[group_rows(0), :], slice(0, 2))
         load(g_raw[0], grad_out[group_rows(0), :], slice(2, 4))
-        load(adj_raw[0][0], adj[group_rows(0), group_rows(0)])
         load(g_raw[1], grad_out[group_rows(1), :])
+        load(adj_raw[0][0], adj[group_rows(0), group_rows(0)])
         load(adj_raw[1][0], adj[group_rows(1), group_rows(0)])
-        load(adj_raw[0][1], adj[group_rows(0), group_rows(1)])
         load(w_raw, W2)
+        load(adj_raw[0][1], adj[group_rows(0), group_rows(1)])
         load(adj_raw[1][1], adj[group_rows(1), group_rows(1)])
         load(h_raw[0], h_ln[group_rows(0), :])
         load(h_raw[1], h_ln[group_rows(1), :])
@@ -213,81 +223,83 @@ def tile_gcnlayer_pb_v_kernel(tc, h_ln, adj, W2, b2, dinv, grad_out, out_0, out_
         nc.scalar.activation(out=ident[:], in_=ident_bf16[:], func=COPY)
         nc.vector.tensor_tensor(out=d_sq[:], in0=d[:], in1=d[:], op=MULT)
 
+        first_half, second_half = slice(0, F // 2), slice(F // 2, F)
         scale_grad(0)
         self_loop(0, range(PACK))
         interleave("vector", dz2_q[0], dz2[0])
-        interleave_adj("vector", 0, 0)
-        self_loop(1, (0, 1))
-        quantize(dz2_q[0])
         scale_grad(1)
-        quantize(adj_q[0][0])
-        aggregate(0, 0)
-        interleave_adj("scalar", 1, 0)
+        self_loop(1, range(PACK))
+        interleave_adj("vector", 0, 0)
+        quantize(dz2_q[0])
         interleave("vector", dz2_q[1], dz2[1])
-        quantize(adj_q[1][0])
-        quantize(dz2_q[1])
-        interleave_adj("scalar", 0, 1)
+        quantize(adj_q[0][0])
         transpose_w(0, 4)
         transpose_w(1, 5)
+        aggregate(0, 0)
+        interleave_adj("scalar", 1, 0)
+        quantize(dz2_q[1])
+        quantize(adj_q[1][0])
+        interleave_adj("scalar", 0, 1)
         aggregate(1, 0)
         interleave_adj("vector", 1, 1)
         collect_w(0, 4)
         collect_w(1, 5)
-        self_loop(1, (2, 3))
+        make_dz1(0, 0)
         quantize(adj_q[0][1])
         aggregate(0, 1)
-        make_dz1(0, 0)
-        quantize(adj_q[1][1])
         make_dz1(0, 1)
-        aggregate(1, 1)
         transpose_dz1(0, 0, 0)
-        interleave("scalar", h_q[0], h_raw[0])
+        quantize(adj_q[1][1])
+        aggregate(1, 1)
+        interleave_h("scalar", 0, slice(0, 3))
         make_dz1(0, 2)
-        make_dz1(0, 3)
-        transpose_dz1(0, 1, 1)
-        interleave("scalar", h_q[1], h_raw[1], slice(0, 48))
         collect_dz1(0, 0, 0)
-        collect_dz1(0, 1, 1)
+        make_dz1(0, 3)
         quantize(w_q)
+        transpose_dz1(0, 1, 1)
+        quantize(dz1_feat_q[0], first_half)
+        dx_matmul(0, 0, 2)
+        dx_matmul(0, 1, 0)
+        interleave("scalar", dz1_node_q[0], dz1[0], slice(0, P // 2))
+        collect_dz1(0, 1, 1)
         make_dz1(1, 0)
         make_dz1(1, 1)
-        quantize(dz1_feat_q[0], slice(0, 256))
-        dx_matmul(0, 0, 2)
-        dx_matmul(0, 1, 3)
+        dx_out("scalar", 0, 0, 2)
+        dx_out("scalar", 0, 1, 0)
         transpose_dz1(1, 0, 4)
-        make_dz1(1, 2)
-        quantize(dz1_feat_q[0], slice(256, 512))
-        dx_matmul(0, 2, 0)
+        quantize(dz1_feat_q[0], second_half)
+        dx_matmul(0, 2, 3)
         dx_matmul(0, 3, 1)
+        make_dz1(1, 2)
         make_dz1(1, 3)
-        transpose_dz1(1, 1, 5)
-        interleave("scalar", h_q[1], h_raw[1], slice(48, 80))
-        for t in range(PACK):
-            dx_out("scalar", 0, t, (t + 2) % 4)
         collect_dz1(1, 0, 4)
+        transpose_dz1(1, 1, 5)
+        dx_out("scalar", 0, 2, 3)
+        dx_out("scalar", 0, 3, 1)
         collect_dz1(1, 1, 5)
-        interleave("vector", dz1_node_q[0], dz1[0])
-        quantize(h_q[0])
-        quantize(dz1_feat_q[1], slice(0, 256))
-        dx_banks = (6, 7, 2, 3)
-        dx_matmul(1, 0, dx_banks[0])
-        dx_matmul(1, 1, dx_banks[1])
-        quantize(dz1_node_q[0])
-        quantize(dz1_feat_q[1], slice(256, 512))
-        dx_matmul(1, 2, dx_banks[2])
-        dx_matmul(1, 3, dx_banks[3])
-        dw_banks = (0, 1, 4, 5)
-        for r in range(PACK):
-            dw_matmul(0, r, dw_banks[r])
-        interleave("scalar", h_q[1], h_raw[1], slice(80, 128))
+        quantize(dz1_feat_q[1], first_half)
+        dx_matmul(1, 0, 6)
+        dx_matmul(1, 1, 7)
+        interleave_h("vector", 1, slice(0, 2))
         interleave("vector", dz1_node_q[1], dz1[1])
-        for t in range(PACK):
-            dx_out("scalar", 1, t, dx_banks[t])
-        quantize(h_q[1], block(0))
+        interleave("scalar", dz1_node_q[0], dz1[0], slice(P // 2, P))
+        quantize(dz1_feat_q[1], second_half)
+        dx_matmul(1, 2, 2)
+        dx_matmul(1, 3, 0)
+        dx_out("scalar", 1, 0, 6)
+        dx_out("scalar", 1, 1, 7)
         quantize(dz1_node_q[1])
-        for r in range(PACK):
-            dw_matmul(1, r, dw_banks[r])
-            if r + 1 < PACK:
-                quantize(h_q[1], block(r + 1))
-        for r in range(PACK):
-            dw_out("scalar" if r % 2 == 0 else "vector", r, dw_banks[r])
+        quantize(dz1_node_q[0])
+        dx_out("scalar", 1, 2, 2)
+        dx_out("scalar", 1, 3, 0)
+        dw_matmuls(0, 3)
+        interleave_h("vector", 1, slice(2, 3))
+        dw_matmuls(1, 1)
+        dw_out("scalar", 0, 3)
+        interleave_h("vector", 0, slice(3, 4))
+        interleave_h("vector", 1, slice(3, 4))
+        dw_matmuls(2, 4)
+        dw_out("scalar", 1, 1)
+        dw_matmuls(3, 5)
+        dw_out("scalar", 2, 4)
+        dw_out("vector", 3, 5)

@@ -91,8 +91,8 @@ def tile_gcnlayer_pb_v_kernel(tc, h_ln, adj, W2, b2, dinv, grad_out, out_0, out_
         def scale_grad(g):
             for t in range(PACK):
                 nc.vector.tensor_scalar(
-                    out=as_halves(dz2[g][:, slot(t)]),
-                    in0=in_halves(g_raw[g][:, slot(t)]),
+                    out=dz2[g][:, slot(t)],
+                    in0=g_raw[g][:, slot(t)],
                     scalar1=d[:, g * PACK + t : g * PACK + t + 1],
                     scalar2=None,
                     op0=MULT,
@@ -112,6 +112,12 @@ def tile_gcnlayer_pb_v_kernel(tc, h_ln, adj, W2, b2, dinv, grad_out, out_0, out_
                 engine,
                 q["values"][:].rearrange("p (c i t) -> p c t i", i=4, t=PACK)[:, runs],
                 src[:].rearrange("p (t c i) -> p c t i", i=4, t=PACK)[:, runs],
+            )
+
+        def interleave_dz2(g):
+            nc.vector.tensor_copy(
+                out=dz2_q[g]["values"][:].rearrange("p (u w e t) -> p w t u e", u=2, e=2, t=PACK),
+                in_=dz2[g][:].rearrange("p (t w u e) -> p w t u e", u=2, e=2, t=PACK),
             )
 
         def interleave_adj(engine, i, j):
@@ -169,8 +175,8 @@ def tile_gcnlayer_pb_v_kernel(tc, h_ln, adj, W2, b2, dinv, grad_out, out_0, out_
 
         def collect_w(half, b):
             nc.scalar.copy(
-                out=w_q["values"][:].bitcast(F32).rearrange("p (n r u) -> p n r u", r=PACK, u=2)[:, :, 2 * half : 2 * half + 2, :],
-                in_=bank[b][:].rearrange("p (r u n) -> p n r u", r=2, u=2),
+                out=w_q["values"][:].bitcast(F32)[:, slot(half)].rearrange("p (r n u) -> p r n u", r=2, u=2),
+                in_=bank[b][:].rearrange("p (r u n) -> p r n u", r=2, u=2),
             )
 
         def transpose_dz1(g, half, b):
@@ -197,13 +203,14 @@ def tile_gcnlayer_pb_v_kernel(tc, h_ln, adj, W2, b2, dinv, grad_out, out_0, out_
             for g in range(GROUPS):
                 matmul(b, h_q, block(r * GROUPS + g), dz1_node_q[g], g == 0, g == GROUPS - 1)
 
-        def dw_out(engine, r, b):
+        def dw_out(engine, r, b, words=slice(0, P)):
             copy_on(
                 engine,
-                dw[:, slot(r)].rearrange("p (w u e) -> p w u e", u=2, e=2),
-                bank[b][:].rearrange("p (u w e) -> p w u e", u=2, e=2),
+                dw[:, slot(r)].rearrange("p (w u e) -> p w u e", u=2, e=2)[:, words],
+                bank[b][:].rearrange("p (u w e) -> p w u e", u=2, e=2)[:, words],
             )
-            nc.sync.dma_start(out=out_1[block(r), :], in_=dw[:, slot(r)])
+            cols = slice(words.start * PACK, words.stop * PACK)
+            nc.sync.dma_start(out=out_1[block(r), cols], in_=dw[:, slot(r)][:, cols])
 
         nc.scalar.dma_start(
             out=d[:].rearrange("p (g t) -> p g t", t=PACK),
@@ -214,7 +221,10 @@ def tile_gcnlayer_pb_v_kernel(tc, h_ln, adj, W2, b2, dinv, grad_out, out_0, out_
         load(g_raw[1], grad_out[group_rows(1), :])
         load(adj_raw[0][0], adj[group_rows(0), group_rows(0)])
         load(adj_raw[1][0], adj[group_rows(1), group_rows(0)])
-        load(w_raw, W2)
+        nc.sync.dma_start(
+            out=w_raw[:].rearrange("p (r c) -> p r c", r=PACK),
+            in_=W2.rearrange("(r p) c -> p r c", r=PACK),
+        )
         load(adj_raw[0][1], adj[group_rows(0), group_rows(1)])
         load(adj_raw[1][1], adj[group_rows(1), group_rows(1)])
         load(h_raw[0], h_ln[group_rows(0), :])
@@ -226,12 +236,12 @@ def tile_gcnlayer_pb_v_kernel(tc, h_ln, adj, W2, b2, dinv, grad_out, out_0, out_
         first_half, second_half = slice(0, F // 2), slice(F // 2, F)
         scale_grad(0)
         self_loop(0, range(PACK))
-        interleave("vector", dz2_q[0], dz2[0])
+        interleave_dz2(0)
         scale_grad(1)
         self_loop(1, range(PACK))
         interleave_adj("vector", 0, 0)
         quantize(dz2_q[0])
-        interleave("vector", dz2_q[1], dz2[1])
+        interleave_dz2(1)
         quantize(adj_q[0][0])
         transpose_w(0, 4)
         transpose_w(1, 5)
@@ -302,4 +312,5 @@ def tile_gcnlayer_pb_v_kernel(tc, h_ln, adj, W2, b2, dinv, grad_out, out_0, out_
         dw_out("scalar", 1, 1)
         dw_matmuls(3, 5)
         dw_out("scalar", 2, 4)
-        dw_out("vector", 3, 5)
+        dw_out("vector", 3, 5, slice(0, P // 2))
+        dw_out("vector", 3, 5, slice(P // 2, P))

from contextlib import ExitStack

import concourse.mybir as mybir
from concourse.masks import make_identity

N, F = 1024, 512
FLOPS = 2 * N * N * F + 2 * N * F * F + 2 * N * F * F
BYTES = 2 * (N * F + N * N + F * F + N * F) + 4 * N + 4 * (N * F + F * F)

F32 = mybir.dt.float32
BF16 = mybir.dt.bfloat16
U32 = mybir.dt.uint32
U8 = mybir.dt.uint8
E4M3 = mybir.dt.float8_e4m3fn_x4
E5M2 = mybir.dt.float8_e5m2_x4
MULT = mybir.AluOpType.mult
ADD = mybir.AluOpType.add
COPY = mybir.ActivationFunctionType.Copy

P = 128
PACK = 4
K_PASS = P * PACK
GROUPS = N // K_PASS
WIDE = PACK * F


def tile_gcnlayer_pb_v_kernel(tc, h_ln, adj, W2, b2, dinv, grad_out, out_0, out_1):
    nc = tc.nc
    with ExitStack() as ctx:
        sb = ctx.enter_context(tc.tile_pool(name="sb", bufs=1))
        ps = ctx.enter_context(tc.psum_pool(name="ps", bufs=1))
        ctx.enter_context(tc.manual_schedule())

        def wide(name, dtype=BF16):
            return sb.tile([P, WIDE], dtype, name=name, align_bytes=64)

        def operand(name, fmt, columns=F):
            values = sb.tile([P, columns * PACK], BF16, name=name + "_values", align_bytes=64)
            codes = sb.tile([P, columns], U32, name=name + "_codes", align_bytes=64)
            scales = sb.tile([P, columns], U8, name=name + "_scales", align_bytes=64)
            return {"values": values, "codes": codes, "scales": scales, "fmt": fmt}

        bank = [ps.tile([P, F], F32, name="bank%d" % b) for b in range(8)]
        ident_bf16 = sb.tile([P, P], BF16, name="ident_bf16")
        ident = sb.tile([P, P], F32, name="ident")
        d = sb.tile([P, GROUPS * PACK], F32, name="d")
        d_sq = sb.tile([P, GROUPS * PACK], F32, name="d_sq")
        g_raw = [wide("g_raw%d" % g) for g in range(GROUPS)]
        h_raw = [wide("h_raw%d" % g) for g in range(GROUPS)]
        adj_raw = [[wide("adj_raw%d%d" % (i, j)) for j in range(GROUPS)] for i in range(GROUPS)]
        w_raw = wide("w_raw")
        dz2 = [wide("dz2_%d" % g) for g in range(GROUPS)]
        loop_term = [wide("loop_term%d" % g, F32) for g in range(GROUPS)]
        dz1 = [wide("dz1_%d" % g) for g in range(GROUPS)]
        dx = [wide("dx%d" % g, F32) for g in range(GROUPS)]
        dw = wide("dw", F32)
        dz2_q = [operand("dz2_q%d" % g, E5M2) for g in range(GROUPS)]
        adj_q = [[operand("adj_q%d%d" % (i, j), E4M3) for j in range(GROUPS)] for i in range(GROUPS)]
        h_q = operand("h_q", E4M3, GROUPS * F)
        w_q = operand("w_q", E4M3)
        dz1_node_q = [operand("dz1_node_q%d" % g, E5M2) for g in range(GROUPS)]
        dz1_feat_q = [operand("dz1_feat_q%d" % g, E5M2) for g in range(GROUPS)]

        def slot(t):
            return slice(t * F, (t + 1) * F)

        def block(t):
            return slice(t * P, (t + 1) * P)

        def group_rows(g):
            return slice(g * K_PASS, (g + 1) * K_PASS)

        def load(tile, rows, slots=slice(0, PACK)):
            nc.sync.dma_start(
                out=tile[:].rearrange("p (t c) -> p t c", t=PACK)[:, slots],
                in_=rows.rearrange("(p t) c -> p t c", t=PACK)[:, slots],
            )

        def copy_on(engine, out, in_):
            if engine == "vector":
                nc.vector.tensor_copy(out=out, in_=in_)
            else:
                nc.scalar.copy(out=out, in_=in_)

        def in_halves(ap):
            return ap.rearrange("p (w u e) -> p u w e", u=2, e=2)

        def as_halves(ap):
            return ap.rearrange("p (u w e) -> p u w e", u=2, e=2)

        def scale_grad(g):
            for t in range(PACK):
                nc.vector.tensor_scalar(
                    out=dz2[g][:, slot(t)],
                    in0=g_raw[g][:, slot(t)],
                    scalar1=d[:, g * PACK + t : g * PACK + t + 1],
                    scalar2=None,
                    op0=MULT,
                )

        def self_loop(g, slots):
            for t in slots:
                nc.scalar.activation(
                    out=as_halves(loop_term[g][:, slot(t)]),
                    in_=in_halves(g_raw[g][:, slot(t)]),
                    func=COPY,
                    scale=d_sq[:, g * PACK + t : g * PACK + t + 1],
                )

        def interleave(engine, q, src, runs=slice(0, P)):
            copy_on(
                engine,
                q["values"][:].rearrange("p (c i t) -> p c t i", i=4, t=PACK)[:, runs],
                src[:].rearrange("p (t c i) -> p c t i", i=4, t=PACK)[:, runs],
            )

        def interleave_dz2(g):
            nc.vector.tensor_copy(
                out=dz2_q[g]["values"][:].rearrange("p (u w e t) -> p w t u e", u=2, e=2, t=PACK),
                in_=dz2[g][:].rearrange("p (t w u e) -> p w t u e", u=2, e=2, t=PACK),
            )

        def interleave_adj(engine, i, j):
            copy_on(
                engine,
                adj_q[i][j]["values"][:].rearrange("p (s a b t) -> p a s b t", s=PACK, b=2, t=PACK),
                adj_raw[i][j][:].rearrange("p (t a b s) -> p a s b t", s=PACK, b=2, t=PACK),
            )

        def interleave_h(engine, g, blocks):
            copy_on(
                engine,
                h_q["values"][:].rearrange("p (r g c i t) -> p r g c t i", r=PACK, g=GROUPS, i=4, t=PACK)[:, blocks, g],
                h_raw[g][:].rearrange("p (t r c i) -> p r c t i", r=PACK, i=4, t=PACK)[:, blocks],
            )

        def quantize(q, cols=slice(0, F)):
            nc.vector.quantize_mx(
                out=q["codes"][:, cols].bitcast(q["fmt"]),
                scales=q["scales"][:, cols],
                in_=q["values"][:, cols.start * PACK : cols.stop * PACK],
            )

        def matmul(b, lhs, cols, rhs, start, stop):
            nc.tensor.matmul_mx(
                out=bank[b][:],
                lhsT=lhs["codes"][:, cols].bitcast(lhs["fmt"]),
                lhsT_scale=lhs["scales"][:, cols],
                rhs=rhs["codes"][:].bitcast(rhs["fmt"]),
                rhs_scale=rhs["scales"][:],
                start=start,
                stop=stop,
            )

        def aggregate(i, j):
            for t in range(PACK):
                matmul(j * PACK + t, adj_q[i][j], block(t), dz2_q[i], i == 0, i == GROUPS - 1)

        def make_dz1(g, t):
            nc.vector.scalar_tensor_tensor(
                out=dz1[g][:, slot(t)],
                in0=bank[g * PACK + t][:],
                scalar=d[:, g * PACK + t : g * PACK + t + 1],
                in1=loop_term[g][:, slot(t)],
                op0=MULT,
                op1=ADD,
            )

        def transpose_w(half, b):
            words = w_raw[:].bitcast(F32)
            for r in range(2):
                base = (2 * half + r) * 2 * P
                for u in range(2):
                    nc.tensor.transpose(bank[b][:, block(2 * r + u)], words[:, base + u : base + 2 * P : 2], ident[:])

        def collect_w(half, b):
            nc.scalar.copy(
                out=w_q["values"][:].bitcast(F32)[:, slot(half)].rearrange("p (r n u) -> p r n u", r=2, u=2),
                in_=bank[b][:].rearrange("p (r u n) -> p r n u", r=2, u=2),
            )

        def transpose_dz1(g, half, b):
            words = dz1[g][:].bitcast(F32)
            for r in range(PACK):
                nc.tensor.transpose(bank[b][:, block(r)], words[:, block(PACK * half + r)], ident[:])

        def collect_dz1(g, half, b):
            nc.scalar.copy(
                out=dz1_feat_q[g]["values"][:].bitcast(F32)[:, slot(half)].rearrange("p (t n u) -> p t n u", t=2, u=2),
                in_=bank[b][:].rearrange("p (t u n) -> p t n u", t=2, u=2),
            )

        def dx_matmul(g, t, b):
            matmul(b, dz1_feat_q[g], block(t), w_q, True, True)

        def dx_out(engine, g, t, b):
            copy_on(engine, dx[g][:, slot(t)], bank[b][:])
            rows = out_0[group_rows(g), :].rearrange("(p t) c -> p t c", t=PACK)
            nc.sync.dma_start(out=rows[:, t, :], in_=dx[g][:, slot(t)])

        def dw_matmuls(r, b):
            quantize(h_q, slice(r * GROUPS * P, (r + 1) * GROUPS * P))
            for g in range(GROUPS):
                matmul(b, h_q, block(r * GROUPS + g), dz1_node_q[g], g == 0, g == GROUPS - 1)

        def dw_out(engine, r, b, words=slice(0, P)):
            copy_on(
                engine,
                dw[:, slot(r)].rearrange("p (w u e) -> p w u e", u=2, e=2)[:, words],
                bank[b][:].rearrange("p (u w e) -> p w u e", u=2, e=2)[:, words],
            )
            cols = slice(words.start * PACK, words.stop * PACK)
            nc.sync.dma_start(out=out_1[block(r), cols], in_=dw[:, slot(r)][:, cols])

        nc.scalar.dma_start(
            out=d[:].rearrange("p (g t) -> p g t", t=PACK),
            in_=dinv.rearrange("(g p t) -> p g t", p=P, t=PACK),
        )
        load(g_raw[0], grad_out[group_rows(0), :], slice(0, 2))
        load(g_raw[0], grad_out[group_rows(0), :], slice(2, 4))
        load(g_raw[1], grad_out[group_rows(1), :])
        load(adj_raw[0][0], adj[group_rows(0), group_rows(0)])
        load(adj_raw[1][0], adj[group_rows(1), group_rows(0)])
        nc.sync.dma_start(
            out=w_raw[:].rearrange("p (r c) -> p r c", r=PACK),
            in_=W2.rearrange("(r p) c -> p r c", r=PACK),
        )
        load(adj_raw[0][1], adj[group_rows(0), group_rows(1)])
        load(adj_raw[1][1], adj[group_rows(1), group_rows(1)])
        load(h_raw[0], h_ln[group_rows(0), :])
        load(h_raw[1], h_ln[group_rows(1), :])
        make_identity(nc, ident_bf16[:])
        nc.scalar.activation(out=ident[:], in_=ident_bf16[:], func=COPY)
        nc.vector.tensor_tensor(out=d_sq[:], in0=d[:], in1=d[:], op=MULT)

        first_half, second_half = slice(0, F // 2), slice(F // 2, F)
        scale_grad(0)
        self_loop(0, range(PACK))
        interleave_dz2(0)
        scale_grad(1)
        self_loop(1, range(PACK))
        interleave_adj("vector", 0, 0)
        quantize(dz2_q[0])
        interleave_dz2(1)
        quantize(adj_q[0][0])
        transpose_w(0, 4)
        transpose_w(1, 5)
        aggregate(0, 0)
        interleave_adj("scalar", 1, 0)
        quantize(dz2_q[1])
        quantize(adj_q[1][0])
        interleave_adj("scalar", 0, 1)
        aggregate(1, 0)
        interleave_adj("vector", 1, 1)
        collect_w(0, 4)
        collect_w(1, 5)
        make_dz1(0, 0)
        quantize(adj_q[0][1])
        aggregate(0, 1)
        make_dz1(0, 1)
        transpose_dz1(0, 0, 0)
        quantize(adj_q[1][1])
        aggregate(1, 1)
        interleave_h("scalar", 0, slice(0, 3))
        make_dz1(0, 2)
        collect_dz1(0, 0, 0)
        make_dz1(0, 3)
        quantize(w_q)
        transpose_dz1(0, 1, 1)
        quantize(dz1_feat_q[0], first_half)
        dx_matmul(0, 0, 2)
        dx_matmul(0, 1, 0)
        interleave("scalar", dz1_node_q[0], dz1[0], slice(0, P // 2))
        collect_dz1(0, 1, 1)
        make_dz1(1, 0)
        make_dz1(1, 1)
        dx_out("scalar", 0, 0, 2)
        dx_out("scalar", 0, 1, 0)
        transpose_dz1(1, 0, 4)
        quantize(dz1_feat_q[0], second_half)
        dx_matmul(0, 2, 3)
        dx_matmul(0, 3, 1)
        make_dz1(1, 2)
        make_dz1(1, 3)
        collect_dz1(1, 0, 4)
        transpose_dz1(1, 1, 5)
        dx_out("scalar", 0, 2, 3)
        dx_out("scalar", 0, 3, 1)
        collect_dz1(1, 1, 5)
        quantize(dz1_feat_q[1], first_half)
        dx_matmul(1, 0, 6)
        dx_matmul(1, 1, 7)
        interleave_h("vector", 1, slice(0, 2))
        interleave("vector", dz1_node_q[1], dz1[1])
        interleave("scalar", dz1_node_q[0], dz1[0], slice(P // 2, P))
        quantize(dz1_feat_q[1], second_half)
        dx_matmul(1, 2, 2)
        dx_matmul(1, 3, 0)
        dx_out("scalar", 1, 0, 6)
        dx_out("scalar", 1, 1, 7)
        quantize(dz1_node_q[1])
        quantize(dz1_node_q[0])
        dx_out("scalar", 1, 2, 2)
        dx_out("scalar", 1, 3, 0)
        dw_matmuls(0, 3)
        interleave_h("vector", 1, slice(2, 3))
        dw_matmuls(1, 1)
        dw_out("scalar", 0, 3)
        interleave_h("vector", 0, slice(3, 4))
        interleave_h("vector", 1, slice(3, 4))
        dw_matmuls(2, 4)
        dw_out("scalar", 1, 1)
        dw_matmuls(3, 5)
        dw_out("scalar", 2, 4)
        dw_out("vector", 3, 5, slice(0, P // 2))
        dw_out("vector", 3, 5, slice(P // 2, P))
